import numpy as np
import ml_dtypes


def mxq(x, axis, fmt="e4m3"):
    dtype, down = {"e4m3": (ml_dtypes.float8_e4m3fn, 7), "e5m2": (ml_dtypes.float8_e5m2, 14)}[fmt]
    v = np.moveaxis(np.asarray(x, np.float32).astype(ml_dtypes.bfloat16).astype(np.float64), axis, -1)
    blocks = v.reshape(v.shape[:-1] + (-1, 32))
    amax = np.abs(blocks).max(-1, keepdims=True)
    byte = np.maximum(np.where(amax > 0, np.frexp(amax)[1] - 1 + 127, 0) - down, 1)
    scale = np.exp2(byte - 127.0)
    codes = (blocks / scale).astype(np.float32).astype(dtype).astype(np.float64)
    return np.moveaxis((codes * scale).reshape(v.shape), -1, axis)


WIDE = False


def mx_kscale(k):
    if not WIDE:
        return np.ones(k)
    levels = np.array([10, -10, 5, -5, 0])
    a = np.random.permutation(np.resize(levels, k // 512 * 4)).reshape(k // 512, 4)
    idx = np.arange(k)
    return np.exp2(a[idx // 512, idx % 128 // 32])


BF16 = ml_dtypes.bfloat16


def bf(x):
    return np.asarray(x, np.float32).astype(BF16)


def f64(x):
    return np.asarray(x).astype(np.float64)


B, D_IN, D_H = 512, 1024, 1024


def sigmoid(v):
    return 1.0 / (1.0 + np.exp(-v))


def setup_inputs():
    s, t = mx_kscale(D_IN), mx_kscale(D_H)

    def w_in():
        return bf(np.random.standard_normal((D_H, D_IN)) * 0.6 / np.sqrt(D_IN) / s[None, :])

    def w_rec():
        return bf(np.random.standard_normal((D_H, D_H)) * 0.6 / np.sqrt(D_H) / t[None, :])

    def bias():
        return bf(np.random.standard_normal(D_H) * 0.3)

    return {"incoming": bf(np.random.standard_normal((B, D_IN)) * s), "h": bf(np.random.standard_normal((B, D_H)) * t),
            "W_i": w_in(), "b_W_i": bias(), "W_c": w_in(), "b_W_c": bias(),
            "U_i": w_rec(), "b_U_i": bias(), "U_c": w_rec(), "b_U_c": bias()}


def reference(incoming, h, W_i, b_W_i, W_c, b_W_c, U_i, b_U_i, U_c, b_U_c):
    xq = mxq(f64(incoming), 1, "e4m3")
    hq = mxq(f64(h), 1, "e4m3")
    I = sigmoid((xq @ mxq(f64(W_i), 1, "e4m3").T) + f64(b_W_i) + (hq @ mxq(f64(U_i), 1, "e4m3").T) + f64(b_U_i))
    C_head = (xq @ mxq(f64(W_c), 1, "e4m3").T) + f64(b_W_c) + (hq @ mxq(f64(U_c), 1, "e4m3").T) + f64(b_U_c)
    return I * C_head

@@ -1,0 +1,211 @@
+from contextlib import ExitStack
+
+import concourse.mybir as mybir
+from concourse.masks import make_identity
+
+F32 = mybir.dt.float32
+BF16 = mybir.dt.bfloat16
+U32 = mybir.dt.uint32
+U8 = mybir.dt.uint8
+FP8X4 = mybir.dt.float8_e4m3fn_x4
+SIGMOID = mybir.ActivationFunctionType.Sigmoid
+ADD = mybir.AluOpType.add
+MULT = mybir.AluOpType.mult
+
+P = 128
+PACK = 4
+BATCH = 512
+FEATURES = 1024
+OUTPUTS = 1024
+PASSES = FEATURES // (P * PACK)
+WORD_BLOCKS = FEATURES // 2 // P
+BATCH_TILES = BATCH // P
+UNITS = OUTPUTS // P
+SOURCES = 2
+GATES = 2
+
+FLOPS = 2 * BATCH * OUTPUTS * FEATURES * SOURCES * GATES
+
+
+def tile_lstmcell_pa_kernel(
+    tc, incoming, h, W_i, b_W_i, W_c, b_W_c, U_i, b_U_i, U_c, b_U_c, out
+):
+    nc = tc.nc
+    activations = (incoming, h)
+    weights = (W_i, U_i, W_c, U_c)
+    biases = (b_W_i, b_U_i, b_W_c, b_U_c)
+
+    with ExitStack() as ctx:
+        ctx.enter_context(tc.manual_schedule())
+
+        const = ctx.enter_context(tc.tile_pool(name="const", bufs=1))
+        act_rows_pool = ctx.enter_context(tc.tile_pool(name="act_rows", bufs=SOURCES))
+        w_rows_pool = ctx.enter_context(tc.tile_pool(name="w_rows", bufs=UNITS))
+        act_grouped_pool = ctx.enter_context(tc.tile_pool(name="act_grouped", bufs=SOURCES))
+        w_grouped_pool = ctx.enter_context(tc.tile_pool(name="w_grouped", bufs=2))
+        w_mx_pool = ctx.enter_context(tc.tile_pool(name="w_mx", bufs=2))
+        result_pool = ctx.enter_context(tc.tile_pool(name="result", bufs=3))
+        word_banks = ctx.enter_context(tc.psum_pool(name="word_banks", bufs=4))
+        sum_banks = ctx.enter_context(tc.psum_pool(name="sum_banks", bufs=1))
+        turned_banks = ctx.enter_context(tc.psum_pool(name="turned_banks", bufs=1))
+
+        act_rows = []
+        for source in range(SOURCES):
+            rows = act_rows_pool.tile([P, BATCH_TILES, FEATURES], BF16, name="act_rows")
+            for bt in range(BATCH_TILES):
+                nc.sync.dma_start(
+                    out=rows[:, bt, :], in_=activations[source][bt * P : (bt + 1) * P, :]
+                )
+            act_rows.append(rows)
+        w_rows = []
+        for unit in range(UNITS):
+            rows = w_rows_pool.tile([P, len(weights), FEATURES], BF16, name="w_rows")
+            for m in range(len(weights)):
+                nc.sync.dma_start(
+                    out=rows[:, m, :], in_=weights[m][unit * P : (unit + 1) * P, :]
+                )
+            w_rows.append(rows)
+
+        bias_rows = const.tile([P, P], BF16, name="bias_rows")
+        nc.vector.memset(bias_rows[:], 0.0)
+        for m in range(len(biases)):
+            nc.scalar.dma_start(
+                out=bias_rows[m * UNITS : (m + 1) * UNITS, :],
+                in_=biases[m].rearrange("(u p) -> u p", p=P),
+            )
+
+        identity = const.tile([P, P], F32, name="identity")
+        make_identity(nc, identity[:])
+
+        warm = const.tile([P, 2], F32, name="warm")
+        nc.vector.memset(warm[:], 0.0)
+        nc.scalar.activation(out=warm[:, 1:2], in_=warm[:, 0:1], func=SIGMOID)
+
+        def transpose_rows(rows_bf16, grouped_words, copy):
+            words = rows_bf16.bitcast(F32)
+            bank = word_banks.tile([P, WORD_BLOCKS, P], F32, name="bank")
+            for v in range(WORD_BLOCKS):
+                nc.tensor.transpose(bank[:, v, :], words[:, v * P : (v + 1) * P], identity[:])
+            copy(out=grouped_words, in_=bank[:].rearrange("p (g u) r -> p g r u", u=2))
+
+        act_codes = const.tile([P, SOURCES, PASSES, BATCH], U32, name="act_codes", align_bytes=64)
+        act_scales = const.tile([P, SOURCES, PASSES, BATCH], U8, name="act_scales", align_bytes=64)
+        for source in range(SOURCES):
+            grouped = act_grouped_pool.tile(
+                [P, PASSES, BATCH, PACK], BF16, name="act_grouped", align_bytes=64
+            )
+            grouped_words = grouped[:].bitcast(F32)
+            for bt in range(BATCH_TILES):
+                transpose_rows(
+                    act_rows[source][:, bt, :],
+                    grouped_words[:, :, bt * P : (bt + 1) * P, :],
+                    nc.vector.tensor_copy if bt % 2 == 0 else nc.scalar.copy,
+                )
+            nc.vector.quantize_mx(
+                out=act_codes[:, source].rearrange("p g b -> p (g b)").bitcast(FP8X4),
+                scales=act_scales[:, source].rearrange("p g b -> p (g b)"),
+                in_=grouped[:].rearrange("p g b t -> p (g b t)"),
+            )
+
+        def transpose_unit(unit):
+            grouped = w_grouped_pool.tile(
+                [P, len(weights), PASSES, P, PACK], BF16, name="w_grouped", align_bytes=64
+            )
+            grouped_words = grouped[:].bitcast(F32)
+            for m in range(len(weights)):
+                transpose_rows(w_rows[unit][:, m, :], grouped_words[:, m], nc.scalar.copy)
+            return grouped
+
+        def quantise_unit(grouped):
+            codes = w_mx_pool.tile(
+                [P, len(weights), PASSES, P], U32, name="w_codes", align_bytes=64
+            )
+            scales = w_mx_pool.tile(
+                [P, len(weights), PASSES, P], U8, name="w_scales", align_bytes=64
+            )
+            for gate in range(GATES):
+                pair = slice(SOURCES * gate, SOURCES * (gate + 1))
+                nc.vector.quantize_mx(
+                    out=codes[:, pair].rearrange("p m g r -> p (m g r)").bitcast(FP8X4),
+                    scales=scales[:, pair].rearrange("p m g r -> p (m g r)"),
+                    in_=grouped[:, pair].rearrange("p m g r t -> p (m g r t)"),
+                )
+            return codes, scales
+
+        def multiply(sums, gate, codes, scales):
+            steps = [(source, g) for source in range(SOURCES) for g in range(PASSES)]
+            for source, g in steps:
+                m = SOURCES * gate + source
+                nc.tensor.matmul_mx(
+                    out=sums[:],
+                    lhsT=codes[:, m, g, :].bitcast(FP8X4),
+                    lhsT_scale=scales[:, m, g, :],
+                    rhs=act_codes[:, source, g, :].bitcast(FP8X4),
+                    rhs_scale=act_scales[:, source, g, :],
+                    start=(source, g) == steps[0],
+                    stop=(source, g) == steps[-1],
+                )
+
+        def turn_product(product):
+            turned = turned_banks.tile([P, BATCH_TILES, P], F32, name="turned")
+            for bt in range(BATCH_TILES):
+                nc.tensor.transpose(turned[:, bt, :], product[:, bt * P : (bt + 1) * P], identity[:])
+            return turned
+
+        def store_product(unit, turned):
+            result = result_pool.tile([P, BATCH_TILES, P], F32, name="result")
+            nc.vector.tensor_copy(out=result[:], in_=turned[:])
+            nc.sync.dma_start(
+                out=out.rearrange("(bt p) n -> p bt n", p=P)[:, :, unit * P : (unit + 1) * P],
+                in_=result[:],
+            )
+
+        first_grouped = transpose_unit(0)
+
+        bias_rows_f32 = const.tile([P, P], F32, name="bias_rows_f32")
+        nc.vector.tensor_copy(out=bias_rows_f32[:], in_=bias_rows[:])
+        bias_bank = turned_banks.tile([P, BATCH_TILES, P], F32, name="turned")
+        nc.tensor.transpose(bias_bank[:, 0, :], bias_rows_f32[:], identity[:])
+        bias_columns = const.tile([P, GATES, SOURCES, UNITS], F32, name="bias_columns")
+        nc.vector.tensor_copy(
+            out=bias_columns[:].rearrange("p g s u -> p (g s u)"),
+            in_=bias_bank[:, 0, 0 : len(biases) * UNITS],
+        )
+        bias = const.tile([P, GATES, UNITS], F32, name="bias")
+        nc.vector.tensor_tensor(
+            out=bias[:], in0=bias_columns[:, :, 0, :], in1=bias_columns[:, :, 1, :], op=ADD
+        )
+
+        mx_operands = quantise_unit(first_grouped)
+        product = None
+        for unit in range(UNITS):
+            last_product = product
+            if unit + 1 < UNITS:
+                next_grouped = transpose_unit(unit + 1)
+
+            codes, scales = mx_operands
+            gate_sums = sum_banks.tile([P, BATCH], F32, name="gate_sums")
+            multiply(gate_sums, 0, codes, scales)
+            gate = result_pool.tile([P, BATCH], F32, name="gate")
+            nc.scalar.activation(
+                out=gate[:], in_=gate_sums[:], func=SIGMOID, bias=bias[:, 0, unit : unit + 1]
+            )
+            candidate_sums = sum_banks.tile([P, BATCH], F32, name="candidate_sums")
+            multiply(candidate_sums, 1, codes, scales)
+            if last_product is not None:
+                turned = turn_product(last_product)
+
+            if unit + 1 < UNITS:
+                mx_operands = quantise_unit(next_grouped)
+            product = result_pool.tile([P, BATCH], F32, name="product")
+            nc.vector.scalar_tensor_tensor(
+                out=product[:],
+                in0=candidate_sums[:],
+                scalar=bias[:, 1, unit : unit + 1],
+                in1=gate[:],
+                op0=ADD,
+                op1=MULT,
+            )
+            if last_product is not None:
+                store_product(unit - 1, turned)
+        store_product(UNITS - 1, turn_product(product))

@@ -23,6 +23,7 @@ BATCH_TILES = BATCH // P
 UNITS = OUTPUTS // P
 SOURCES = 2
 GATES = 2
+BLOCK = 32
 
 FLOPS = 2 * BATCH * OUTPUTS * FEATURES * SOURCES * GATES
 
@@ -45,9 +46,8 @@ def tile_lstmcell_pa_kernel(
         w_grouped_pool = ctx.enter_context(tc.tile_pool(name="w_grouped", bufs=2))
         w_mx_pool = ctx.enter_context(tc.tile_pool(name="w_mx", bufs=2))
         result_pool = ctx.enter_context(tc.tile_pool(name="result", bufs=3))
-        word_banks = ctx.enter_context(tc.psum_pool(name="word_banks", bufs=4))
+        word_banks = ctx.enter_context(tc.psum_pool(name="word_banks", bufs=6))
         sum_banks = ctx.enter_context(tc.psum_pool(name="sum_banks", bufs=1))
-        turned_banks = ctx.enter_context(tc.psum_pool(name="turned_banks", bufs=1))
 
         act_rows = []
         for source in range(SOURCES):
@@ -146,25 +146,23 @@ def tile_lstmcell_pa_kernel(
                     stop=(source, g) == steps[-1],
                 )
 
-        def turn_product(product):
-            turned = turned_banks.tile([P, BATCH_TILES, P], F32, name="turned")
-            for bt in range(BATCH_TILES):
-                nc.tensor.transpose(turned[:, bt, :], product[:, bt * P : (bt + 1) * P], identity[:])
-            return turned
-
-        def store_product(unit, turned):
-            result = result_pool.tile([P, BATCH_TILES, P], F32, name="result")
-            nc.vector.tensor_copy(out=result[:], in_=turned[:])
-            nc.sync.dma_start(
-                out=out.rearrange("(bt p) n -> p bt n", p=P)[:, :, unit * P : (unit + 1) * P],
-                in_=result[:],
-            )
+        def store_product(unit, product):
+            turned = result_pool.tile([P, BATCH], F32, name="turned", align_bytes=64)
+            nc.vector.transpose(out=turned[:], in_=product[:])
+            for a in range(P // BLOCK):
+                first = unit * P + a * BLOCK
+                nc.sync.dma_start(
+                    out=out.rearrange("(c i) n -> i c n", i=BLOCK)[:, :, first : first + BLOCK],
+                    in_=turned[a * BLOCK : (a + 1) * BLOCK, :].rearrange(
+                        "i (c j) -> i c j", j=BLOCK
+                    ),
+                )
 
         first_grouped = transpose_unit(0)
 
         bias_rows_f32 = const.tile([P, P], F32, name="bias_rows_f32")
         nc.vector.tensor_copy(out=bias_rows_f32[:], in_=bias_rows[:])
-        bias_bank = turned_banks.tile([P, BATCH_TILES, P], F32, name="turned")
+        bias_bank = word_banks.tile([P, WORD_BLOCKS, P], F32, name="bank")
         nc.tensor.transpose(bias_bank[:, 0, :], bias_rows_f32[:], identity[:])
         bias_columns = const.tile([P, GATES, SOURCES, UNITS], F32, name="bias_columns")
         nc.vector.tensor_copy(
@@ -192,12 +190,12 @@ def tile_lstmcell_pa_kernel(
             )
             candidate_sums = sum_banks.tile([P, BATCH], F32, name="candidate_sums")
             multiply(candidate_sums, 1, codes, scales)
-            if last_product is not None:
-                turned = turn_product(last_product)
 
+            if last_product is not None:
+                store_product(unit - 1, last_product)
             if unit + 1 < UNITS:
                 mx_operands = quantise_unit(next_grouped)
-            product = result_pool.tile([P, BATCH], F32, name="product")
+            product = result_pool.tile([P, BATCH], F32, name="product", align_bytes=64)
             nc.vector.scalar_tensor_tensor(
                 out=product[:],
                 in0=candidate_sums[:],
@@ -206,6 +204,4 @@ def tile_lstmcell_pa_kernel(
                 op0=ADD,
                 op1=MULT,
             )
-            if last_product is not None:
-                store_product(unit - 1, turned)
-        store_product(UNITS - 1, turn_product(product))
+        store_product(UNITS - 1, product)

@@ -33,8 +33,8 @@ def tile_lstmcell_pa_kernel(
 ):
     nc = tc.nc
     activations = (incoming, h)
-    weights = (W_i, U_i, W_c, U_c)
-    biases = (b_W_i, b_U_i, b_W_c, b_U_c)
+    weights = (W_i, W_c, U_i, U_c)
+    biases = (b_W_i, b_W_c, b_U_i, b_U_c)
 
     with ExitStack() as ctx:
         ctx.enter_context(tc.manual_schedule())
@@ -49,22 +49,27 @@ def tile_lstmcell_pa_kernel(
         word_banks = ctx.enter_context(tc.psum_pool(name="word_banks", bufs=6))
         sum_banks = ctx.enter_context(tc.psum_pool(name="sum_banks", bufs=1))
 
-        act_rows = []
-        for source in range(SOURCES):
+        def load_activation(source):
             rows = act_rows_pool.tile([P, BATCH_TILES, FEATURES], BF16, name="act_rows")
             for bt in range(BATCH_TILES):
                 nc.sync.dma_start(
                     out=rows[:, bt, :], in_=activations[source][bt * P : (bt + 1) * P, :]
                 )
-            act_rows.append(rows)
-        w_rows = []
-        for unit in range(UNITS):
+            return rows
+
+        def load_unit(unit):
             rows = w_rows_pool.tile([P, len(weights), FEATURES], BF16, name="w_rows")
             for m in range(len(weights)):
                 nc.sync.dma_start(
                     out=rows[:, m, :], in_=weights[m][unit * P : (unit + 1) * P, :]
                 )
-            w_rows.append(rows)
+            return rows
+
+        act_rows = [load_activation(0)]
+        w_rows = [load_unit(0)]
+        act_rows.append(load_activation(1))
+        for unit in range(1, UNITS):
+            w_rows.append(load_unit(unit))
 
         bias_rows = const.tile([P, P], BF16, name="bias_rows")
         nc.vector.memset(bias_rows[:], 0.0)
@@ -90,7 +95,8 @@ def tile_lstmcell_pa_kernel(
 
         act_codes = const.tile([P, SOURCES, PASSES, BATCH], U32, name="act_codes", align_bytes=64)
         act_scales = const.tile([P, SOURCES, PASSES, BATCH], U8, name="act_scales", align_bytes=64)
-        for source in range(SOURCES):
+
+        def prepare_activation(source):
             grouped = act_grouped_pool.tile(
                 [P, PASSES, BATCH, PACK], BF16, name="act_grouped", align_bytes=64
             )
@@ -101,11 +107,12 @@ def tile_lstmcell_pa_kernel(
                     grouped_words[:, :, bt * P : (bt + 1) * P, :],
                     nc.vector.tensor_copy if bt % 2 == 0 else nc.scalar.copy,
                 )
-            nc.vector.quantize_mx(
-                out=act_codes[:, source].rearrange("p g b -> p (g b)").bitcast(FP8X4),
-                scales=act_scales[:, source].rearrange("p g b -> p (g b)"),
-                in_=grouped[:].rearrange("p g b t -> p (g b t)"),
-            )
+            for g in range(PASSES):
+                nc.vector.quantize_mx(
+                    out=act_codes[:, source, g, :].bitcast(FP8X4),
+                    scales=act_scales[:, source, g, :],
+                    in_=grouped[:, g].rearrange("p b t -> p (b t)"),
+                )
 
         def transpose_unit(unit):
             grouped = w_grouped_pool.tile(
@@ -123,8 +130,8 @@ def tile_lstmcell_pa_kernel(
             scales = w_mx_pool.tile(
                 [P, len(weights), PASSES, P], U8, name="w_scales", align_bytes=64
             )
-            for gate in range(GATES):
-                pair = slice(SOURCES * gate, SOURCES * (gate + 1))
+            for source in range(SOURCES):
+                pair = slice(GATES * source, GATES * (source + 1))
                 nc.vector.quantize_mx(
                     out=codes[:, pair].rearrange("p m g r -> p (m g r)").bitcast(FP8X4),
                     scales=scales[:, pair].rearrange("p m g r -> p (m g r)"),
@@ -132,19 +139,42 @@ def tile_lstmcell_pa_kernel(
                 )
             return codes, scales
 
-        def multiply(sums, gate, codes, scales):
-            steps = [(source, g) for source in range(SOURCES) for g in range(PASSES)]
-            for source, g in steps:
-                m = SOURCES * gate + source
-                nc.tensor.matmul_mx(
-                    out=sums[:],
-                    lhsT=codes[:, m, g, :].bitcast(FP8X4),
-                    lhsT_scale=scales[:, m, g, :],
-                    rhs=act_codes[:, source, g, :].bitcast(FP8X4),
-                    rhs_scale=act_scales[:, source, g, :],
-                    start=(source, g) == steps[0],
-                    stop=(source, g) == steps[-1],
-                )
+        def new_sums():
+            gate_sums = sum_banks.tile([P, BATCH], F32, name="gate_sums")
+            candidate_sums = sum_banks.tile([P, BATCH], F32, name="candidate_sums")
+            return gate_sums, candidate_sums
+
+        def multiply(sums, source, mx_operands):
+            codes, scales = mx_operands
+            for gate in range(GATES):
+                m = GATES * source + gate
+                for g in range(PASSES):
+                    nc.tensor.matmul_mx(
+                        out=sums[gate][:],
+                        lhsT=codes[:, m, g, :].bitcast(FP8X4),
+                        lhsT_scale=scales[:, m, g, :],
+                        rhs=act_codes[:, source, g, :].bitcast(FP8X4),
+                        rhs_scale=act_scales[:, source, g, :],
+                        start=(source == 0 and g == 0),
+                        stop=(source == SOURCES - 1 and g == PASSES - 1),
+                    )
+
+        def gate_times_candidate(unit, sums):
+            gate_sums, candidate_sums = sums
+            gate = result_pool.tile([P, BATCH], F32, name="gate")
+            nc.scalar.activation(
+                out=gate[:], in_=gate_sums[:], func=SIGMOID, bias=bias[:, 0, unit : unit + 1]
+            )
+            product = result_pool.tile([P, BATCH], F32, name="product", align_bytes=64)
+            nc.vector.scalar_tensor_tensor(
+                out=product[:],
+                in0=candidate_sums[:],
+                scalar=bias[:, 1, unit : unit + 1],
+                in1=gate[:],
+                op0=ADD,
+                op1=MULT,
+            )
+            return product
 
         def store_product(unit, product):
             turned = result_pool.tile([P, BATCH], F32, name="turned", align_bytes=64)
@@ -158,50 +188,40 @@ def tile_lstmcell_pa_kernel(
                     ),
                 )
 
-        first_grouped = transpose_unit(0)
+        prepare_activation(0)
+        mx_operands = quantise_unit(transpose_unit(0))
+        sums = new_sums()
+        multiply(sums, 0, mx_operands)
 
         bias_rows_f32 = const.tile([P, P], F32, name="bias_rows_f32")
         nc.vector.tensor_copy(out=bias_rows_f32[:], in_=bias_rows[:])
         bias_bank = word_banks.tile([P, WORD_BLOCKS, P], F32, name="bank")
         nc.tensor.transpose(bias_bank[:, 0, :], bias_rows_f32[:], identity[:])
-        bias_columns = const.tile([P, GATES, SOURCES, UNITS], F32, name="bias_columns")
+        bias_columns = const.tile([P, SOURCES, GATES, UNITS], F32, name="bias_columns")
         nc.vector.tensor_copy(
-            out=bias_columns[:].rearrange("p g s u -> p (g s u)"),
+            out=bias_columns[:].rearrange("p s g u -> p (s g u)"),
             in_=bias_bank[:, 0, 0 : len(biases) * UNITS],
         )
         bias = const.tile([P, GATES, UNITS], F32, name="bias")
         nc.vector.tensor_tensor(
-            out=bias[:], in0=bias_columns[:, :, 0, :], in1=bias_columns[:, :, 1, :], op=ADD
+            out=bias[:], in0=bias_columns[:, 0], in1=bias_columns[:, 1], op=ADD
         )
 
-        mx_operands = quantise_unit(first_grouped)
+        prepare_activation(1)
+
         product = None
         for unit in range(UNITS):
             last_product = product
             if unit + 1 < UNITS:
                 next_grouped = transpose_unit(unit + 1)
-
-            codes, scales = mx_operands
-            gate_sums = sum_banks.tile([P, BATCH], F32, name="gate_sums")
-            multiply(gate_sums, 0, codes, scales)
-            gate = result_pool.tile([P, BATCH], F32, name="gate")
-            nc.scalar.activation(
-                out=gate[:], in_=gate_sums[:], func=SIGMOID, bias=bias[:, 0, unit : unit + 1]
-            )
-            candidate_sums = sum_banks.tile([P, BATCH], F32, name="candidate_sums")
-            multiply(candidate_sums, 1, codes, scales)
+            if unit > 0:
+                sums = new_sums()
+                multiply(sums, 0, mx_operands)
+            multiply(sums, 1, mx_operands)
 
             if last_product is not None:
                 store_product(unit - 1, last_product)
             if unit + 1 < UNITS:
                 mx_operands = quantise_unit(next_grouped)
-            product = result_pool.tile([P, BATCH], F32, name="product", align_bytes=64)
-            nc.vector.scalar_tensor_tensor(
-                out=product[:],
-                in0=candidate_sums[:],
-                scalar=bias[:, 1, unit : unit + 1],
-                in1=gate[:],
-                op0=ADD,
-                op1=MULT,
-            )
+            product = gate_times_candidate(unit, sums)
         store_product(UNITS - 1, product)

from contextlib import ExitStack

import concourse.mybir as mybir
from concourse.masks import make_identity

F32 = mybir.dt.float32
BF16 = mybir.dt.bfloat16
U32 = mybir.dt.uint32
U8 = mybir.dt.uint8
FP8X4 = mybir.dt.float8_e4m3fn_x4
SIGMOID = mybir.ActivationFunctionType.Sigmoid
ADD = mybir.AluOpType.add
MULT = mybir.AluOpType.mult

P = 128
PACK = 4
BATCH = 512
FEATURES = 1024
OUTPUTS = 1024
PASSES = FEATURES // (P * PACK)
WORD_BLOCKS = FEATURES // 2 // P
BATCH_TILES = BATCH // P
UNITS = OUTPUTS // P
SOURCES = 2
GATES = 2
BLOCK = 32

FLOPS = 2 * BATCH * OUTPUTS * FEATURES * SOURCES * GATES


def tile_lstmcell_pa_kernel(
    tc, incoming, h, W_i, b_W_i, W_c, b_W_c, U_i, b_U_i, U_c, b_U_c, out
):
    nc = tc.nc
    activations = (incoming, h)
    weights = (W_i, W_c, U_i, U_c)
    biases = (b_W_i, b_W_c, b_U_i, b_U_c)

    with ExitStack() as ctx:
        ctx.enter_context(tc.manual_schedule())

        const = ctx.enter_context(tc.tile_pool(name="const", bufs=1))
        act_rows_pool = ctx.enter_context(tc.tile_pool(name="act_rows", bufs=SOURCES))
        w_rows_pool = ctx.enter_context(tc.tile_pool(name="w_rows", bufs=UNITS))
        act_grouped_pool = ctx.enter_context(tc.tile_pool(name="act_grouped", bufs=SOURCES))
        w_grouped_pool = ctx.enter_context(tc.tile_pool(name="w_grouped", bufs=2))
        w_mx_pool = ctx.enter_context(tc.tile_pool(name="w_mx", bufs=2))
        result_pool = ctx.enter_context(tc.tile_pool(name="result", bufs=3))
        word_banks = ctx.enter_context(tc.psum_pool(name="word_banks", bufs=6))
        sum_banks = ctx.enter_context(tc.psum_pool(name="sum_banks", bufs=1))

        def load_activation(source):
            rows = act_rows_pool.tile([P, BATCH_TILES, FEATURES], BF16, name="act_rows")
            for bt in range(BATCH_TILES):
                nc.sync.dma_start(
                    out=rows[:, bt, :], in_=activations[source][bt * P : (bt + 1) * P, :]
                )
            return rows

        def load_unit(unit):
            rows = w_rows_pool.tile([P, len(weights), FEATURES], BF16, name="w_rows")
            for m in range(len(weights)):
                nc.sync.dma_start(
                    out=rows[:, m, :], in_=weights[m][unit * P : (unit + 1) * P, :]
                )
            return rows

        act_rows = [load_activation(0)]
        w_rows = [load_unit(0)]
        act_rows.append(load_activation(1))
        for unit in range(1, UNITS):
            w_rows.append(load_unit(unit))

        bias_rows = const.tile([P, P], BF16, name="bias_rows")
        nc.vector.memset(bias_rows[:], 0.0)
        for m in range(len(biases)):
            nc.scalar.dma_start(
                out=bias_rows[m * UNITS : (m + 1) * UNITS, :],
                in_=biases[m].rearrange("(u p) -> u p", p=P),
            )

        identity = const.tile([P, P], F32, name="identity")
        make_identity(nc, identity[:])

        warm = const.tile([P, 2], F32, name="warm")
        nc.vector.memset(warm[:], 0.0)
        nc.scalar.activation(out=warm[:, 1:2], in_=warm[:, 0:1], func=SIGMOID)

        def transpose_rows(rows_bf16, grouped_words, copy):
            words = rows_bf16.bitcast(F32)
            bank = word_banks.tile([P, WORD_BLOCKS, P], F32, name="bank")
            for v in range(WORD_BLOCKS):
                nc.tensor.transpose(bank[:, v, :], words[:, v * P : (v + 1) * P], identity[:])
            copy(out=grouped_words, in_=bank[:].rearrange("p (g u) r -> p g r u", u=2))

        act_codes = const.tile([P, SOURCES, PASSES, BATCH], U32, name="act_codes", align_bytes=64)
        act_scales = const.tile([P, SOURCES, PASSES, BATCH], U8, name="act_scales", align_bytes=64)

        def prepare_activation(source):
            grouped = act_grouped_pool.tile(
                [P, PASSES, BATCH, PACK], BF16, name="act_grouped", align_bytes=64
            )
            grouped_words = grouped[:].bitcast(F32)
            for bt in range(BATCH_TILES):
                transpose_rows(
                    act_rows[source][:, bt, :],
                    grouped_words[:, :, bt * P : (bt + 1) * P, :],
                    nc.vector.tensor_copy if bt % 2 == 0 else nc.scalar.copy,
                )
            for g in range(PASSES):
                nc.vector.quantize_mx(
                    out=act_codes[:, source, g, :].bitcast(FP8X4),
                    scales=act_scales[:, source, g, :],
                    in_=grouped[:, g].rearrange("p b t -> p (b t)"),
                )

        def transpose_unit(unit):
            grouped = w_grouped_pool.tile(
                [P, len(weights), PASSES, P, PACK], BF16, name="w_grouped", align_bytes=64
            )
            grouped_words = grouped[:].bitcast(F32)
            for m in range(len(weights)):
                transpose_rows(w_rows[unit][:, m, :], grouped_words[:, m], nc.scalar.copy)
            return grouped

        def quantise_unit(grouped):
            codes = w_mx_pool.tile(
                [P, len(weights), PASSES, P], U32, name="w_codes", align_bytes=64
            )
            scales = w_mx_pool.tile(
                [P, len(weights), PASSES, P], U8, name="w_scales", align_bytes=64
            )
            for source in range(SOURCES):
                pair = slice(GATES * source, GATES * (source + 1))
                nc.vector.quantize_mx(
                    out=codes[:, pair].rearrange("p m g r -> p (m g r)").bitcast(FP8X4),
                    scales=scales[:, pair].rearrange("p m g r -> p (m g r)"),
                    in_=grouped[:, pair].rearrange("p m g r t -> p (m g r t)"),
                )
            return codes, scales

        def new_sums():
            gate_sums = sum_banks.tile([P, BATCH], F32, name="gate_sums")
            candidate_sums = sum_banks.tile([P, BATCH], F32, name="candidate_sums")
            return gate_sums, candidate_sums

        def multiply(sums, source, mx_operands):
            codes, scales = mx_operands
            for gate in range(GATES):
                m = GATES * source + gate
                for g in range(PASSES):
                    nc.tensor.matmul_mx(
                        out=sums[gate][:],
                        lhsT=codes[:, m, g, :].bitcast(FP8X4),
                        lhsT_scale=scales[:, m, g, :],
                        rhs=act_codes[:, source, g, :].bitcast(FP8X4),
                        rhs_scale=act_scales[:, source, g, :],
                        start=(source == 0 and g == 0),
                        stop=(source == SOURCES - 1 and g == PASSES - 1),
                    )

        def gate_times_candidate(unit, sums):
            gate_sums, candidate_sums = sums
            gate = result_pool.tile([P, BATCH], F32, name="gate")
            nc.scalar.activation(
                out=gate[:], in_=gate_sums[:], func=SIGMOID, bias=bias[:, 0, unit : unit + 1]
            )
            product = result_pool.tile([P, BATCH], F32, name="product", align_bytes=64)
            nc.vector.scalar_tensor_tensor(
                out=product[:],
                in0=candidate_sums[:],
                scalar=bias[:, 1, unit : unit + 1],
                in1=gate[:],
                op0=ADD,
                op1=MULT,
            )
            return product

        def store_product(unit, product):
            turned = result_pool.tile([P, BATCH], F32, name="turned", align_bytes=64)
            nc.vector.transpose(out=turned[:], in_=product[:])
            for a in range(P // BLOCK):
                first = unit * P + a * BLOCK
                nc.sync.dma_start(
                    out=out.rearrange("(c i) n -> i c n", i=BLOCK)[:, :, first : first + BLOCK],
                    in_=turned[a * BLOCK : (a + 1) * BLOCK, :].rearrange(
                        "i (c j) -> i c j", j=BLOCK
                    ),
                )

        prepare_activation(0)
        mx_operands = quantise_unit(transpose_unit(0))
        sums = new_sums()
        multiply(sums, 0, mx_operands)

        bias_rows_f32 = const.tile([P, P], F32, name="bias_rows_f32")
        nc.vector.tensor_copy(out=bias_rows_f32[:], in_=bias_rows[:])
        bias_bank = word_banks.tile([P, WORD_BLOCKS, P], F32, name="bank")
        nc.tensor.transpose(bias_bank[:, 0, :], bias_rows_f32[:], identity[:])
        bias_columns = const.tile([P, SOURCES, GATES, UNITS], F32, name="bias_columns")
        nc.vector.tensor_copy(
            out=bias_columns[:].rearrange("p s g u -> p (s g u)"),
            in_=bias_bank[:, 0, 0 : len(biases) * UNITS],
        )
        bias = const.tile([P, GATES, UNITS], F32, name="bias")
        nc.vector.tensor_tensor(
            out=bias[:], in0=bias_columns[:, 0], in1=bias_columns[:, 1], op=ADD
        )

        prepare_activation(1)

        product = None
        for unit in range(UNITS):
            last_product = product
            if unit + 1 < UNITS:
                next_grouped = transpose_unit(unit + 1)
            if unit > 0:
                sums = new_sums()
                multiply(sums, 0, mx_operands)
            multiply(sums, 1, mx_operands)

            if last_product is not None:
                store_product(unit - 1, last_product)
            if unit + 1 < UNITS:
                mx_operands = quantise_unit(next_grouped)
            product = gate_times_candidate(unit, sums)
        store_product(UNITS - 1, product)
